import numpy as np
import ml_dtypes


def mxq(x, axis, fmt="e4m3"):
    dtype, down = {"e4m3": (ml_dtypes.float8_e4m3fn, 7), "e5m2": (ml_dtypes.float8_e5m2, 14)}[fmt]
    v = np.moveaxis(np.asarray(x, np.float32).astype(ml_dtypes.bfloat16).astype(np.float64), axis, -1)
    blocks = v.reshape(v.shape[:-1] + (-1, 32))
    amax = np.abs(blocks).max(-1, keepdims=True)
    byte = np.maximum(np.where(amax > 0, np.frexp(amax)[1] - 1 + 127, 0) - down, 1)
    scale = np.exp2(byte - 127.0)
    codes = (blocks / scale).astype(np.float32).astype(dtype).astype(np.float64)
    return np.moveaxis((codes * scale).reshape(v.shape), -1, axis)


WIDE = False


def mx_kscale(k):
    if not WIDE:
        return np.ones(k)
    levels = np.array([10, -10, 5, -5, 0])
    a = np.random.permutation(np.resize(levels, k // 512 * 4)).reshape(k // 512, 4)
    idx = np.arange(k)
    return np.exp2(a[idx // 512, idx % 128 // 32])


BF16 = ml_dtypes.bfloat16


def bf(x):
    return np.asarray(x, np.float32).astype(BF16)


def f64(x):
    return np.asarray(x).astype(np.float64)


E2M1 = np.array([0.0, 0.5, 1.0, 1.5, 2.0, 3.0, 4.0, 6.0, -0.0, -0.5, -1.0, -1.5, -2.0, -3.0, -4.0, -6.0])


def pack_weight(w, fmt):
    k, n = w.shape
    w = f64(bf(w)).reshape(k // 32, 32, n)
    amax = np.abs(w).max(1)
    if fmt == "e4m3":
        byte = np.frexp(amax)[1] - 1 + 127 - 7
    else:
        mant, ex = np.frexp(amax / 6.0)
        byte = np.where(mant > 0.5, ex, ex - 1) + 127
    byte = np.clip(np.where(amax > 0, byte, 1), 1, 254)
    scaled = (w * np.exp2(127.0 - byte)[:, None, :]).reshape(k, n).astype(np.float32)
    by_word = np.ascontiguousarray(scaled.reshape(k // 512, 128, 4, n).transpose(0, 1, 3, 2))
    if fmt == "e4m3":
        words = by_word.astype(ml_dtypes.float8_e4m3fn).view(np.uint8)
    else:
        c = by_word.astype(ml_dtypes.float4_e2m1fn).view(np.uint8) & 0xF
        words = c[..., 0::2] | (c[..., 1::2] << 4)
    return np.ascontiguousarray(words), np.ascontiguousarray(byte.astype(np.uint8).reshape(k // 512, 16, n))


def unpack_weight(words, scales, fmt):
    g, p, n, _ = words.shape
    if fmt == "e4m3":
        vals = np.ascontiguousarray(words).view(ml_dtypes.float8_e4m3fn).astype(np.float64)
    else:
        nib = np.empty((g, p, n, 4), np.uint8)
        nib[..., 0::2] = words & 0xF
        nib[..., 1::2] = words >> 4
        vals = E2M1[nib]
    vals = vals * np.repeat(np.exp2(scales.astype(np.float64) - 127.0), 8, axis=1)[..., None]
    return vals.transpose(0, 1, 3, 2).reshape(g * 512, n)


B, C, CI, N = 32, 512, 512, 256
A = np.sqrt(0.2 * N / np.sqrt(CI))
FMT = "e4m3"


def conv1x1(w, b, v):
    return (w @ mxq(v, 1, "e4m3")) + b[:, None]


def setup_inputs():
    s, u, t = mx_kscale(C), mx_kscale(C), mx_kscale(CI)
    r = np.random.standard_normal
    x = bf(r((B, C, N)) * s[None, :, None])
    x_2 = bf(r((B, C, N)) * u[None, :, None])
    theta_w = r((CI, C)) * A / np.sqrt(C) * t[:, None] / s[None, :]
    theta_b = bf(r(CI) * 0.2 * A * t)
    phi_w = r((CI, C)) * A / np.sqrt(C) / t[:, None] / u[None, :]
    phi_b = bf(r(CI) * 0.2 * A / t)
    theta_w_words, theta_w_scales = pack_weight(np.ascontiguousarray(theta_w.T), FMT)
    phi_w_words, phi_w_scales = pack_weight(np.ascontiguousarray(phi_w.T), FMT)
    return {"x": x,
            "x_2": x_2,
            "theta_w_words": theta_w_words,
            "theta_w_scales": theta_w_scales,
            "theta_b": theta_b,
            "phi_w_words": phi_w_words,
            "phi_w_scales": phi_w_scales,
            "phi_b": phi_b}


def reference(x, x_2, theta_w_words, theta_w_scales, theta_b, phi_w_words, phi_w_scales, phi_b):
    theta_w = unpack_weight(theta_w_words, theta_w_scales, FMT).T
    phi_w = unpack_weight(phi_w_words, phi_w_scales, FMT).T
    theta_x = conv1x1(theta_w, f64(theta_b), f64(x)).transpose(0, 2, 1)
    phi_x = conv1x1(phi_w, f64(phi_b), f64(x_2))
    return (mxq(theta_x, 2, "e4m3") @ mxq(phi_x, 1, "e4m3")) / N

@@ -1,0 +1,190 @@
+from contextlib import ExitStack
+
+import concourse.mybir as mybir
+from concourse.masks import make_identity
+
+BF16 = mybir.dt.bfloat16
+F32 = mybir.dt.float32
+I32 = mybir.dt.int32
+U32 = mybir.dt.uint32
+U8 = mybir.dt.uint8
+FP8X4 = mybir.dt.float8_e4m3fn_x4
+ACT = mybir.ActivationFunctionType
+
+P = 128
+PACK = 4
+BATCHES = 32
+CHANNELS = P * PACK
+POINTS = 256
+ROUND_B = 2
+ROUNDS = BATCHES // ROUND_B
+COLS = ROUND_B * POINTS
+RUN = 4
+LOADS_AHEAD = 3
+
+FLOPS = 2 * BATCHES * POINTS * CHANNELS * (2 * CHANNELS + POINTS)
+
+
+def load_weight(nc, words, scales, codes_sb, plane_sb):
+    nc.sync.dma_start(
+        out=codes_sb.bitcast(I32),
+        in_=words[0].rearrange("p n t -> p (n t)").bitcast(I32),
+    )
+    for quadrant in range(4):
+        nc.sync.dma_start(
+            out=plane_sb[32 * quadrant : 32 * quadrant + 4, :].bitcast(I32),
+            in_=scales[0, 4 * quadrant : 4 * quadrant + 4, :].bitcast(I32),
+        )
+
+
+def regroup(nc, pool, rows, kind):
+    grouped = pool.tile(
+        [P, ROUND_B, POINTS, PACK], BF16, align_bytes=64, name="grouped_" + kind, tag="grouped_" + kind
+    )
+    nc.vector.tensor_copy(
+        out=grouped[:].rearrange("p b (c i) j -> p b c j i", i=RUN),
+        in_=rows.rearrange("p b j (c i) -> p b c j i", i=RUN),
+    )
+    return grouped
+
+
+def quantise(nc, pool, grouped, kind):
+    codes = pool.tile([P, COLS], U32, align_bytes=64, name="codes_" + kind, tag="codes_" + kind)
+    scales = pool.tile([P, COLS], U8, align_bytes=64, name="scales_" + kind, tag="scales_" + kind)
+    nc.vector.quantize_mx(
+        out=codes[:].bitcast(FP8X4),
+        scales=scales[:],
+        in_=grouped[:].rearrange("p b n j -> p (b n j)"),
+    )
+    return codes, scales
+
+
+def tile_sgcam_pa_t_kernel(
+    tc, x, x_2, theta_w_words, theta_w_scales, theta_b, phi_w_words, phi_w_scales, phi_b, out
+):
+    nc = tc.nc
+    kinds = ("theta", "phi")
+    inputs = {"theta": x, "phi": x_2}
+
+    with ExitStack() as ctx:
+        consts = ctx.enter_context(tc.tile_pool(name="consts", bufs=1))
+        raw_pool = ctx.enter_context(tc.tile_pool(name="raw", bufs=LOADS_AHEAD + 1))
+        work = ctx.enter_context(tc.tile_pool(name="work", bufs=2))
+        planes_pool = ctx.enter_context(tc.tile_pool(name="planes", bufs=3))
+        result_pool = ctx.enter_context(tc.tile_pool(name="result", bufs=3))
+
+        raw = {}
+        in_mx = {}
+        planes = {}
+        feat_mx = {}
+
+        def load_round(r):
+            for kind in kinds:
+                tile_in = raw_pool.tile([P, ROUND_B, PACK, POINTS], BF16, name="raw_" + kind, tag="raw_" + kind)
+                nc.sync.dma_start(
+                    out=tile_in[:].rearrange("p b j n -> p b (j n)"),
+                    in_=inputs[kind][ROUND_B * r : ROUND_B * (r + 1)].rearrange("b (p j) n -> p b (j n)", j=PACK),
+                )
+                raw[kind, r] = tile_in
+
+        load_round(0)
+        w_codes = {}
+        w_planes = {}
+        for kind in kinds:
+            w_codes[kind] = consts.tile([P, CHANNELS], U32, align_bytes=64, name="w_codes_" + kind)
+            w_planes[kind] = consts.tile([P, CHANNELS], U8, align_bytes=64, name="w_planes_" + kind)
+            nc.vector.memset(w_planes[kind][:].bitcast(I32), 0)
+        load_weight(nc, theta_w_words, theta_w_scales, w_codes["theta"][:], w_planes["theta"])
+        load_weight(nc, phi_w_words, phi_w_scales, w_codes["phi"][:], w_planes["phi"])
+        for r in range(1, LOADS_AHEAD):
+            load_round(r)
+
+        identity = consts.tile([P, P], BF16, name="identity")
+        make_identity(nc, identity[:])
+        bias_rows = consts.tile([P, P], BF16, name="bias_rows")
+        nc.vector.memset(bias_rows[:], 0.0)
+        nc.scalar.dma_start(out=bias_rows[0:PACK, :], in_=theta_b.rearrange("(t p) -> t p", p=P))
+        nc.scalar.dma_start(out=bias_rows[PACK : 2 * PACK, :], in_=phi_b.rearrange("(t p) -> t p", p=P))
+        bias = consts.tile([P, 2 * PACK], F32, name="bias")
+        with tc.psum_pool(name="setup_psum", bufs=1) as setup_psum:
+            bias_cols = setup_psum.tile([P, P], BF16, name="bias_cols")
+            nc.tensor.transpose(bias_cols[:], bias_rows[:], identity[:])
+            nc.vector.tensor_copy(out=bias[:], in_=bias_cols[:, 0 : 2 * PACK])
+
+        feat_psum = ctx.enter_context(tc.psum_pool(name="feat_psum", bufs=6))
+        out_psum = ctx.enter_context(tc.psum_pool(name="out_psum", bufs=2))
+
+        def quantise_inputs(r):
+            grouped = {}
+            for kind in kinds:
+                grouped[kind] = regroup(nc, work, raw[kind, r][:], "in_" + kind)
+            for kind in kinds:
+                in_mx[kind, r] = quantise(nc, work, grouped[kind], "in_" + kind)
+
+        def project(r):
+            for k, kind in enumerate(kinds):
+                codes, scales = in_mx[kind, r]
+                feat = planes_pool.tile([P, PACK, ROUND_B, POINTS], BF16, name="planes_" + kind, tag="planes_" + kind)
+                for t in range(PACK):
+                    chans = slice(P * t, P * (t + 1))
+                    acc = feat_psum.tile([P, COLS], F32, name="acc", tag="acc")
+                    nc.tensor.matmul_mx(
+                        out=acc[:],
+                        lhsT=w_codes[kind][:, chans].bitcast(FP8X4),
+                        lhsT_scale=w_planes[kind][:, chans],
+                        rhs=codes[:].bitcast(FP8X4),
+                        rhs_scale=scales[:],
+                        start=True,
+                        stop=True,
+                    )
+                    nc.scalar.activation(
+                        out=feat[:, t].rearrange("p b n -> p (b n)"),
+                        in_=acc[:],
+                        func=ACT.Identity,
+                        bias=bias[:, PACK * k + t : PACK * k + t + 1],
+                        scale=1.0,
+                    )
+                planes[kind, r] = feat
+
+        def quantise_features(r):
+            grouped = {}
+            for kind in kinds:
+                grouped[kind] = regroup(nc, work, planes[kind, r][:].rearrange("p t b n -> p b t n"), "feat_" + kind)
+            for kind in kinds:
+                feat_mx[kind, r] = quantise(nc, work, grouped[kind], "feat_" + kind)
+
+        def affinity(r):
+            th_codes, th_scales = feat_mx["theta", r]
+            ph_codes, ph_scales = feat_mx["phi", r]
+            result = result_pool.tile([P, ROUND_B, POINTS // P, POINTS], F32, name="result")
+            for i in range(ROUND_B):
+                cols = slice(POINTS * i, POINTS * (i + 1))
+                prod = out_psum.tile([P, POINTS // P, POINTS], F32, name="prod")
+                for c in range(POINTS // P):
+                    rows = slice(POINTS * i + P * c, POINTS * i + P * (c + 1))
+                    nc.tensor.matmul_mx(
+                        out=prod[:, c, :],
+                        lhsT=th_codes[:, rows].bitcast(FP8X4),
+                        lhsT_scale=th_scales[:, rows],
+                        rhs=ph_codes[:, cols].bitcast(FP8X4),
+                        rhs_scale=ph_scales[:, cols],
+                        start=True,
+                        stop=True,
+                    )
+                nc.scalar.activation(out=result[:, i], in_=prod[:], func=ACT.Copy, scale=1.0 / POINTS)
+            nc.sync.dma_start(
+                out=out[ROUND_B * r : ROUND_B * (r + 1)].rearrange("b (c p) m -> p b c m", p=P),
+                in_=result[:],
+            )
+
+        with tc.manual_schedule():
+            quantise_inputs(0)
+            project(0)
+            for r in range(ROUNDS):
+                if r + LOADS_AHEAD < ROUNDS:
+                    load_round(r + LOADS_AHEAD)
+                if r + 1 < ROUNDS:
+                    quantise_inputs(r + 1)
+                    project(r + 1)
+                quantise_features(r)
+                affinity(r)

@@ -21,6 +21,7 @@ ROUNDS = BATCHES // ROUND_B
 COLS = ROUND_B * POINTS
 RUN = 4
 LOADS_AHEAD = 3
+SCALAR_EVERY = 4
 
 FLOPS = 2 * BATCHES * POINTS * CHANNELS * (2 * CHANNELS + POINTS)
 
@@ -37,14 +38,17 @@ def load_weight(nc, words, scales, codes_sb, plane_sb):
         )
 
 
-def regroup(nc, pool, rows, kind):
+def regroup(nc, pool, rows, kind, on_scalar=False):
     grouped = pool.tile(
         [P, ROUND_B, POINTS, PACK], BF16, align_bytes=64, name="grouped_" + kind, tag="grouped_" + kind
     )
-    nc.vector.tensor_copy(
-        out=grouped[:].rearrange("p b (c i) j -> p b c j i", i=RUN),
-        in_=rows.rearrange("p b j (c i) -> p b c j i", i=RUN),
-    )
+    dst = grouped[:].rearrange("p b (c i) j -> p b c j i", i=RUN)
+    src = rows.rearrange("p b j (c i) -> p b c j i", i=RUN)
+    if on_scalar:
+        for b in range(ROUND_B):
+            nc.scalar.copy(out=dst[:, b], in_=src[:, b])
+    else:
+        nc.vector.tensor_copy(out=dst, in_=src)
     return grouped
 
 
@@ -74,6 +78,7 @@ def tile_sgcam_pa_t_kernel(
         result_pool = ctx.enter_context(tc.tile_pool(name="result", bufs=3))
 
         raw = {}
+        in_grouped = {}
         in_mx = {}
         planes = {}
         feat_mx = {}
@@ -114,12 +119,16 @@ def tile_sgcam_pa_t_kernel(
         feat_psum = ctx.enter_context(tc.psum_pool(name="feat_psum", bufs=6))
         out_psum = ctx.enter_context(tc.psum_pool(name="out_psum", bufs=2))
 
+        def scalar_regroups(r):
+            if r < ROUNDS and r % SCALAR_EVERY == 0:
+                in_grouped["phi", r] = regroup(nc, work, raw["phi", r][:], "in_phi", on_scalar=True)
+
         def quantise_inputs(r):
-            grouped = {}
             for kind in kinds:
-                grouped[kind] = regroup(nc, work, raw[kind, r][:], "in_" + kind)
+                if (kind, r) not in in_grouped:
+                    in_grouped[kind, r] = regroup(nc, work, raw[kind, r][:], "in_" + kind)
             for kind in kinds:
-                in_mx[kind, r] = quantise(nc, work, grouped[kind], "in_" + kind)
+                in_mx[kind, r] = quantise(nc, work, in_grouped[kind, r], "in_" + kind)
 
         def project(r):
             for k, kind in enumerate(kinds):
@@ -178,6 +187,8 @@ def tile_sgcam_pa_t_kernel(
             )
 
         with tc.manual_schedule():
+            scalar_regroups(0)
+            scalar_regroups(1)
             quantise_inputs(0)
             project(0)
             for r in range(ROUNDS):
@@ -188,3 +199,4 @@ def tile_sgcam_pa_t_kernel(
                     project(r + 1)
                 quantise_features(r)
                 affinity(r)
+                scalar_regroups(r + 2)

@@ -20,8 +20,8 @@ ROUND_B = 2
 ROUNDS = BATCHES // ROUND_B
 COLS = ROUND_B * POINTS
 RUN = 4
-LOADS_AHEAD = 3
-SCALAR_EVERY = 4
+LOADS_AHEAD = 4
+SCALAR_EVERY = 3
 
 FLOPS = 2 * BATCHES * POINTS * CHANNELS * (2 * CHANNELS + POINTS)
 
@@ -121,7 +121,7 @@ def tile_sgcam_pa_t_kernel(
 
         def scalar_regroups(r):
             if r < ROUNDS and r % SCALAR_EVERY == 0:
-                in_grouped["phi", r] = regroup(nc, work, raw["phi", r][:], "in_phi", on_scalar=True)
+                in_grouped["phi", r] = regroup(nc, work, raw["phi", r][:], "in_phi_by_scalar", on_scalar=True)
 
         def quantise_inputs(r):
             for kind in kinds:
@@ -188,9 +188,10 @@ def tile_sgcam_pa_t_kernel(
 
         with tc.manual_schedule():
             scalar_regroups(0)
-            scalar_regroups(1)
             quantise_inputs(0)
             project(0)
+            scalar_regroups(1)
+            scalar_regroups(2)
             for r in range(ROUNDS):
                 if r + LOADS_AHEAD < ROUNDS:
                     load_round(r + LOADS_AHEAD)
@@ -199,4 +200,4 @@ def tile_sgcam_pa_t_kernel(
                     project(r + 1)
                 quantise_features(r)
                 affinity(r)
-                scalar_regroups(r + 2)
+                scalar_regroups(r + 3)

@@ -186,18 +186,17 @@ def tile_sgcam_pa_t_kernel(
                 in_=result[:],
             )
 
-        with tc.manual_schedule():
-            scalar_regroups(0)
-            quantise_inputs(0)
-            project(0)
-            scalar_regroups(1)
-            scalar_regroups(2)
-            for r in range(ROUNDS):
-                if r + LOADS_AHEAD < ROUNDS:
-                    load_round(r + LOADS_AHEAD)
-                if r + 1 < ROUNDS:
-                    quantise_inputs(r + 1)
-                    project(r + 1)
-                quantise_features(r)
-                affinity(r)
-                scalar_regroups(r + 3)
+        scalar_regroups(0)
+        quantise_inputs(0)
+        project(0)
+        scalar_regroups(1)
+        scalar_regroups(2)
+        for r in range(ROUNDS):
+            if r + LOADS_AHEAD < ROUNDS:
+                load_round(r + LOADS_AHEAD)
+            if r + 1 < ROUNDS:
+                quantise_inputs(r + 1)
+                project(r + 1)
+            quantise_features(r)
+            affinity(r)
+            scalar_regroups(r + 3)

@@ -16,49 +16,39 @@ PACK = 4
 BATCHES = 32
 CHANNELS = P * PACK
 POINTS = 256
+SIDES = 2
 ROUND_B = 2
 ROUNDS = BATCHES // ROUND_B
 COLS = ROUND_B * POINTS
+ROW_TILES = POINTS // P
 RUN = 4
-LOADS_AHEAD = 4
 SCALAR_EVERY = 3
+LEAD = 2
+SCALAR_LEAD = LEAD + 2
+LOADS_AHEAD = SCALAR_LEAD + 1
 
 FLOPS = 2 * BATCHES * POINTS * CHANNELS * (2 * CHANNELS + POINTS)
 
 
-def load_weight(nc, words, scales, codes_sb, plane_sb):
-    nc.sync.dma_start(
-        out=codes_sb.bitcast(I32),
-        in_=words[0].rearrange("p n t -> p (n t)").bitcast(I32),
-    )
-    for quadrant in range(4):
-        nc.sync.dma_start(
-            out=plane_sb[32 * quadrant : 32 * quadrant + 4, :].bitcast(I32),
-            in_=scales[0, 4 * quadrant : 4 * quadrant + 4, :].bitcast(I32),
-        )
-
-
-def regroup(nc, pool, rows, kind, on_scalar=False):
-    grouped = pool.tile(
-        [P, ROUND_B, POINTS, PACK], BF16, align_bytes=64, name="grouped_" + kind, tag="grouped_" + kind
-    )
-    dst = grouped[:].rearrange("p b (c i) j -> p b c j i", i=RUN)
-    src = rows.rearrange("p b j (c i) -> p b c j i", i=RUN)
+def regroup(nc, pool, rows, name, on_scalar=False):
+    grouped = pool.tile([P, 2, POINTS, PACK], BF16, align_bytes=64, name=name)
+    src = rows.rearrange("p g j (c i) -> p g c j i", i=RUN)
+    dst = grouped[:].rearrange("p g (c i) j -> p g c j i", i=RUN)
     if on_scalar:
-        for b in range(ROUND_B):
-            nc.scalar.copy(out=dst[:, b], in_=src[:, b])
+        for g in range(2):
+            nc.scalar.copy(out=dst[:, g], in_=src[:, g])
     else:
         nc.vector.tensor_copy(out=dst, in_=src)
     return grouped
 
 
-def quantise(nc, pool, grouped, kind):
-    codes = pool.tile([P, COLS], U32, align_bytes=64, name="codes_" + kind, tag="codes_" + kind)
-    scales = pool.tile([P, COLS], U8, align_bytes=64, name="scales_" + kind, tag="scales_" + kind)
+def quantise(nc, pool, grouped, name):
+    codes = pool.tile([P, 2, POINTS], U32, align_bytes=64, name="codes_" + name)
+    scales = pool.tile([P, 2, POINTS], U8, align_bytes=64, name="scales_" + name)
     nc.vector.quantize_mx(
-        out=codes[:].bitcast(FP8X4),
-        scales=scales[:],
-        in_=grouped[:].rearrange("p b n j -> p (b n j)"),
+        out=codes[:].rearrange("p g n -> p (g n)").bitcast(FP8X4),
+        scales=scales[:].rearrange("p g n -> p (g n)"),
+        in_=grouped[:].rearrange("p g n j -> p (g n j)"),
     )
     return codes, scales
 
@@ -67,40 +57,48 @@ def tile_sgcam_pa_t_kernel(
     tc, x, x_2, theta_w_words, theta_w_scales, theta_b, phi_w_words, phi_w_scales, phi_b, out
 ):
     nc = tc.nc
-    kinds = ("theta", "phi")
-    inputs = {"theta": x, "phi": x_2}
+    inputs = (x, x_2)
+    weight_words = (theta_w_words, phi_w_words)
+    weight_scales = (theta_w_scales, phi_w_scales)
+    biases = (theta_b, phi_b)
+    side_names = ("theta", "phi")
 
     with ExitStack() as ctx:
         consts = ctx.enter_context(tc.tile_pool(name="consts", bufs=1))
         raw_pool = ctx.enter_context(tc.tile_pool(name="raw", bufs=LOADS_AHEAD + 1))
         work = ctx.enter_context(tc.tile_pool(name="work", bufs=2))
-        planes_pool = ctx.enter_context(tc.tile_pool(name="planes", bufs=3))
-        result_pool = ctx.enter_context(tc.tile_pool(name="result", bufs=3))
+        planes_pool = ctx.enter_context(tc.tile_pool(name="planes", bufs=LEAD + 2))
+        result_pool = ctx.enter_context(tc.tile_pool(name="result", bufs=4))
 
         raw = {}
-        in_grouped = {}
-        in_mx = {}
+        grouped_in = {}
+        mx_in = {}
         planes = {}
-        feat_mx = {}
 
         def load_round(r):
-            for kind in kinds:
-                tile_in = raw_pool.tile([P, ROUND_B, PACK, POINTS], BF16, name="raw_" + kind, tag="raw_" + kind)
+            if r >= ROUNDS:
+                return
+            for side in range(SIDES):
+                raw[side, r] = raw_pool.tile([P, ROUND_B, PACK, POINTS], BF16, name="raw_" + side_names[side])
                 nc.sync.dma_start(
-                    out=tile_in[:].rearrange("p b j n -> p b (j n)"),
-                    in_=inputs[kind][ROUND_B * r : ROUND_B * (r + 1)].rearrange("b (p j) n -> p b (j n)", j=PACK),
+                    out=raw[side, r][:].rearrange("p b j n -> p b (j n)"),
+                    in_=inputs[side][ROUND_B * r : ROUND_B * (r + 1)].rearrange("b (p j) n -> p b (j n)", j=PACK),
                 )
-                raw[kind, r] = tile_in
 
         load_round(0)
-        w_codes = {}
-        w_planes = {}
-        for kind in kinds:
-            w_codes[kind] = consts.tile([P, CHANNELS], U32, align_bytes=64, name="w_codes_" + kind)
-            w_planes[kind] = consts.tile([P, CHANNELS], U8, align_bytes=64, name="w_planes_" + kind)
-            nc.vector.memset(w_planes[kind][:].bitcast(I32), 0)
-        load_weight(nc, theta_w_words, theta_w_scales, w_codes["theta"][:], w_planes["theta"])
-        load_weight(nc, phi_w_words, phi_w_scales, w_codes["phi"][:], w_planes["phi"])
+        w_codes = consts.tile([P, SIDES, CHANNELS], U32, align_bytes=64, name="w_codes")
+        w_planes = consts.tile([P, SIDES, CHANNELS], U8, align_bytes=64, name="w_planes")
+        nc.vector.memset(w_planes[:].rearrange("p s c -> p (s c)").bitcast(I32), 0)
+        for side in range(SIDES):
+            nc.sync.dma_start(
+                out=w_codes[:, side].bitcast(I32),
+                in_=weight_words[side][0].rearrange("p n t -> p (n t)").bitcast(I32),
+            )
+            for quadrant in range(4):
+                nc.sync.dma_start(
+                    out=w_planes[32 * quadrant : 32 * quadrant + 4, side].bitcast(I32),
+                    in_=weight_scales[side][0, 4 * quadrant : 4 * quadrant + 4, :].bitcast(I32),
+                )
         for r in range(1, LOADS_AHEAD):
             load_round(r)
 
@@ -108,95 +106,89 @@ def tile_sgcam_pa_t_kernel(
         make_identity(nc, identity[:])
         bias_rows = consts.tile([P, P], BF16, name="bias_rows")
         nc.vector.memset(bias_rows[:], 0.0)
-        nc.scalar.dma_start(out=bias_rows[0:PACK, :], in_=theta_b.rearrange("(t p) -> t p", p=P))
-        nc.scalar.dma_start(out=bias_rows[PACK : 2 * PACK, :], in_=phi_b.rearrange("(t p) -> t p", p=P))
-        bias = consts.tile([P, 2 * PACK], F32, name="bias")
+        for side in range(SIDES):
+            nc.scalar.dma_start(
+                out=bias_rows[PACK * side : PACK * (side + 1), :], in_=biases[side].rearrange("(t p) -> t p", p=P)
+            )
+        bias = consts.tile([P, SIDES * PACK], F32, name="bias")
         with tc.psum_pool(name="setup_psum", bufs=1) as setup_psum:
             bias_cols = setup_psum.tile([P, P], BF16, name="bias_cols")
             nc.tensor.transpose(bias_cols[:], bias_rows[:], identity[:])
-            nc.vector.tensor_copy(out=bias[:], in_=bias_cols[:, 0 : 2 * PACK])
+            nc.vector.tensor_copy(out=bias[:], in_=bias_cols[:, 0 : SIDES * PACK])
 
         feat_psum = ctx.enter_context(tc.psum_pool(name="feat_psum", bufs=6))
         out_psum = ctx.enter_context(tc.psum_pool(name="out_psum", bufs=2))
 
         def scalar_regroups(r):
             if r < ROUNDS and r % SCALAR_EVERY == 0:
-                in_grouped["phi", r] = regroup(nc, work, raw["phi", r][:], "in_phi_by_scalar", on_scalar=True)
+                grouped_in[1, r] = regroup(nc, work, raw[1, r][:], "grouped_by_scalar", on_scalar=True)
 
         def quantise_inputs(r):
-            for kind in kinds:
-                if (kind, r) not in in_grouped:
-                    in_grouped[kind, r] = regroup(nc, work, raw[kind, r][:], "in_" + kind)
-            for kind in kinds:
-                in_mx[kind, r] = quantise(nc, work, in_grouped[kind, r], "in_" + kind)
+            for side in range(SIDES):
+                if (side, r) not in grouped_in:
+                    grouped_in[side, r] = regroup(nc, work, raw[side, r][:], "grouped_" + side_names[side])
+            for side in range(SIDES):
+                mx_in[side, r] = quantise(nc, work, grouped_in[side, r], side_names[side])
 
         def project(r):
-            for k, kind in enumerate(kinds):
-                codes, scales = in_mx[kind, r]
-                feat = planes_pool.tile([P, PACK, ROUND_B, POINTS], BF16, name="planes_" + kind, tag="planes_" + kind)
+            planes[r] = planes_pool.tile([P, PACK, SIDES, ROUND_B, POINTS], BF16, name="planes")
+            for side in range(SIDES):
+                codes, scales = mx_in[side, r]
                 for t in range(PACK):
                     chans = slice(P * t, P * (t + 1))
-                    acc = feat_psum.tile([P, COLS], F32, name="acc", tag="acc")
+                    acc = feat_psum.tile([P, COLS], F32, name="acc")
                     nc.tensor.matmul_mx(
                         out=acc[:],
-                        lhsT=w_codes[kind][:, chans].bitcast(FP8X4),
-                        lhsT_scale=w_planes[kind][:, chans],
-                        rhs=codes[:].bitcast(FP8X4),
-                        rhs_scale=scales[:],
+                        lhsT=w_codes[:, side, chans].bitcast(FP8X4),
+                        lhsT_scale=w_planes[:, side, chans],
+                        rhs=codes[:].rearrange("p b n -> p (b n)").bitcast(FP8X4),
+                        rhs_scale=scales[:].rearrange("p b n -> p (b n)"),
                         start=True,
                         stop=True,
                     )
                     nc.scalar.activation(
-                        out=feat[:, t].rearrange("p b n -> p (b n)"),
+                        out=planes[r][:, t, side].rearrange("p b n -> p (b n)"),
                         in_=acc[:],
                         func=ACT.Identity,
-                        bias=bias[:, PACK * k + t : PACK * k + t + 1],
+                        bias=bias[:, PACK * side + t : PACK * side + t + 1],
                         scale=1.0,
                     )
-                planes[kind, r] = feat
-
-        def quantise_features(r):
-            grouped = {}
-            for kind in kinds:
-                grouped[kind] = regroup(nc, work, planes[kind, r][:].rearrange("p t b n -> p b t n"), "feat_" + kind)
-            for kind in kinds:
-                feat_mx[kind, r] = quantise(nc, work, grouped[kind], "feat_" + kind)
 
         def affinity(r):
-            th_codes, th_scales = feat_mx["theta", r]
-            ph_codes, ph_scales = feat_mx["phi", r]
-            result = result_pool.tile([P, ROUND_B, POINTS // P, POINTS], F32, name="result")
+            grouped = []
             for i in range(ROUND_B):
-                cols = slice(POINTS * i, POINTS * (i + 1))
-                prod = out_psum.tile([P, POINTS // P, POINTS], F32, name="prod")
-                for c in range(POINTS // P):
-                    rows = slice(POINTS * i + P * c, POINTS * i + P * (c + 1))
+                rows = planes[r][:, :, :, i, :].rearrange("p t s n -> p s t n")
+                grouped.append(regroup(nc, work, rows, "grouped_batch%d" % i))
+            for i in range(ROUND_B):
+                codes, scales = quantise(nc, work, grouped[i], "batch%d" % i)
+                prod = out_psum.tile([P, ROW_TILES, POINTS], F32, name="prod")
+                for c in range(ROW_TILES):
+                    rows_c = slice(P * c, P * (c + 1))
                     nc.tensor.matmul_mx(
                         out=prod[:, c, :],
-                        lhsT=th_codes[:, rows].bitcast(FP8X4),
-                        lhsT_scale=th_scales[:, rows],
-                        rhs=ph_codes[:, cols].bitcast(FP8X4),
-                        rhs_scale=ph_scales[:, cols],
+                        lhsT=codes[:, 0, rows_c].bitcast(FP8X4),
+                        lhsT_scale=scales[:, 0, rows_c],
+                        rhs=codes[:, 1, :].bitcast(FP8X4),
+                        rhs_scale=scales[:, 1, :],
                         start=True,
                         stop=True,
                     )
-                nc.scalar.activation(out=result[:, i], in_=prod[:], func=ACT.Copy, scale=1.0 / POINTS)
-            nc.sync.dma_start(
-                out=out[ROUND_B * r : ROUND_B * (r + 1)].rearrange("b (c p) m -> p b c m", p=P),
-                in_=result[:],
-            )
+                result = result_pool.tile([P, ROW_TILES, POINTS], F32, name="result")
+                nc.scalar.activation(out=result[:], in_=prod[:], func=ACT.Copy, scale=1.0 / POINTS)
+                nc.sync.dma_start(out=out[ROUND_B * r + i].rearrange("(c p) m -> p c m", p=P), in_=result[:])
 
-        scalar_regroups(0)
-        quantise_inputs(0)
-        project(0)
-        scalar_regroups(1)
-        scalar_regroups(2)
-        for r in range(ROUNDS):
-            if r + LOADS_AHEAD < ROUNDS:
+        with tc.manual_schedule():
+            scalar_regroups(0)
+            for r in range(LEAD):
+                quantise_inputs(r)
+                project(r)
+                scalar_regroups(r + 1)
+            for r in range(LEAD + 1, SCALAR_LEAD):
+                scalar_regroups(r)
+            for r in range(ROUNDS):
                 load_round(r + LOADS_AHEAD)
-            if r + 1 < ROUNDS:
-                quantise_inputs(r + 1)
-                project(r + 1)
-            quantise_features(r)
-            affinity(r)
-            scalar_regroups(r + 3)
+                if r + LEAD < ROUNDS:
+                    quantise_inputs(r + LEAD)
+                    project(r + LEAD)
+                affinity(r)
+                scalar_regroups(r + SCALAR_LEAD)

from contextlib import ExitStack

import concourse.mybir as mybir
from concourse.masks import make_identity

BF16 = mybir.dt.bfloat16
F32 = mybir.dt.float32
I32 = mybir.dt.int32
U32 = mybir.dt.uint32
U8 = mybir.dt.uint8
FP8X4 = mybir.dt.float8_e4m3fn_x4
ACT = mybir.ActivationFunctionType

P = 128
PACK = 4
BATCHES = 32
CHANNELS = P * PACK
POINTS = 256
SIDES = 2
ROUND_B = 2
ROUNDS = BATCHES // ROUND_B
COLS = ROUND_B * POINTS
ROW_TILES = POINTS // P
RUN = 4
SCALAR_EVERY = 3
LEAD = 2
SCALAR_LEAD = LEAD + 2
LOADS_AHEAD = SCALAR_LEAD + 1

FLOPS = 2 * BATCHES * POINTS * CHANNELS * (2 * CHANNELS + POINTS)


def regroup(nc, pool, rows, name, on_scalar=False):
    grouped = pool.tile([P, 2, POINTS, PACK], BF16, align_bytes=64, name=name)
    src = rows.rearrange("p g j (c i) -> p g c j i", i=RUN)
    dst = grouped[:].rearrange("p g (c i) j -> p g c j i", i=RUN)
    if on_scalar:
        for g in range(2):
            nc.scalar.copy(out=dst[:, g], in_=src[:, g])
    else:
        nc.vector.tensor_copy(out=dst, in_=src)
    return grouped


def quantise(nc, pool, grouped, name):
    codes = pool.tile([P, 2, POINTS], U32, align_bytes=64, name="codes_" + name)
    scales = pool.tile([P, 2, POINTS], U8, align_bytes=64, name="scales_" + name)
    nc.vector.quantize_mx(
        out=codes[:].rearrange("p g n -> p (g n)").bitcast(FP8X4),
        scales=scales[:].rearrange("p g n -> p (g n)"),
        in_=grouped[:].rearrange("p g n j -> p (g n j)"),
    )
    return codes, scales


def tile_sgcam_pa_t_kernel(
    tc, x, x_2, theta_w_words, theta_w_scales, theta_b, phi_w_words, phi_w_scales, phi_b, out
):
    nc = tc.nc
    inputs = (x, x_2)
    weight_words = (theta_w_words, phi_w_words)
    weight_scales = (theta_w_scales, phi_w_scales)
    biases = (theta_b, phi_b)
    side_names = ("theta", "phi")

    with ExitStack() as ctx:
        consts = ctx.enter_context(tc.tile_pool(name="consts", bufs=1))
        raw_pool = ctx.enter_context(tc.tile_pool(name="raw", bufs=LOADS_AHEAD + 1))
        work = ctx.enter_context(tc.tile_pool(name="work", bufs=2))
        planes_pool = ctx.enter_context(tc.tile_pool(name="planes", bufs=LEAD + 2))
        result_pool = ctx.enter_context(tc.tile_pool(name="result", bufs=4))

        raw = {}
        grouped_in = {}
        mx_in = {}
        planes = {}

        def load_round(r):
            if r >= ROUNDS:
                return
            for side in range(SIDES):
                raw[side, r] = raw_pool.tile([P, ROUND_B, PACK, POINTS], BF16, name="raw_" + side_names[side])
                nc.sync.dma_start(
                    out=raw[side, r][:].rearrange("p b j n -> p b (j n)"),
                    in_=inputs[side][ROUND_B * r : ROUND_B * (r + 1)].rearrange("b (p j) n -> p b (j n)", j=PACK),
                )

        load_round(0)
        w_codes = consts.tile([P, SIDES, CHANNELS], U32, align_bytes=64, name="w_codes")
        w_planes = consts.tile([P, SIDES, CHANNELS], U8, align_bytes=64, name="w_planes")
        nc.vector.memset(w_planes[:].rearrange("p s c -> p (s c)").bitcast(I32), 0)
        for side in range(SIDES):
            nc.sync.dma_start(
                out=w_codes[:, side].bitcast(I32),
                in_=weight_words[side][0].rearrange("p n t -> p (n t)").bitcast(I32),
            )
            for quadrant in range(4):
                nc.sync.dma_start(
                    out=w_planes[32 * quadrant : 32 * quadrant + 4, side].bitcast(I32),
                    in_=weight_scales[side][0, 4 * quadrant : 4 * quadrant + 4, :].bitcast(I32),
                )
        for r in range(1, LOADS_AHEAD):
            load_round(r)

        identity = consts.tile([P, P], BF16, name="identity")
        make_identity(nc, identity[:])
        bias_rows = consts.tile([P, P], BF16, name="bias_rows")
        nc.vector.memset(bias_rows[:], 0.0)
        for side in range(SIDES):
            nc.scalar.dma_start(
                out=bias_rows[PACK * side : PACK * (side + 1), :], in_=biases[side].rearrange("(t p) -> t p", p=P)
            )
        bias = consts.tile([P, SIDES * PACK], F32, name="bias")
        with tc.psum_pool(name="setup_psum", bufs=1) as setup_psum:
            bias_cols = setup_psum.tile([P, P], BF16, name="bias_cols")
            nc.tensor.transpose(bias_cols[:], bias_rows[:], identity[:])
            nc.vector.tensor_copy(out=bias[:], in_=bias_cols[:, 0 : SIDES * PACK])

        feat_psum = ctx.enter_context(tc.psum_pool(name="feat_psum", bufs=6))
        out_psum = ctx.enter_context(tc.psum_pool(name="out_psum", bufs=2))

        def scalar_regroups(r):
            if r < ROUNDS and r % SCALAR_EVERY == 0:
                grouped_in[1, r] = regroup(nc, work, raw[1, r][:], "grouped_by_scalar", on_scalar=True)

        def quantise_inputs(r):
            for side in range(SIDES):
                if (side, r) not in grouped_in:
                    grouped_in[side, r] = regroup(nc, work, raw[side, r][:], "grouped_" + side_names[side])
            for side in range(SIDES):
                mx_in[side, r] = quantise(nc, work, grouped_in[side, r], side_names[side])

        def project(r):
            planes[r] = planes_pool.tile([P, PACK, SIDES, ROUND_B, POINTS], BF16, name="planes")
            for side in range(SIDES):
                codes, scales = mx_in[side, r]
                for t in range(PACK):
                    chans = slice(P * t, P * (t + 1))
                    acc = feat_psum.tile([P, COLS], F32, name="acc")
                    nc.tensor.matmul_mx(
                        out=acc[:],
                        lhsT=w_codes[:, side, chans].bitcast(FP8X4),
                        lhsT_scale=w_planes[:, side, chans],
                        rhs=codes[:].rearrange("p b n -> p (b n)").bitcast(FP8X4),
                        rhs_scale=scales[:].rearrange("p b n -> p (b n)"),
                        start=True,
                        stop=True,
                    )
                    nc.scalar.activation(
                        out=planes[r][:, t, side].rearrange("p b n -> p (b n)"),
                        in_=acc[:],
                        func=ACT.Identity,
                        bias=bias[:, PACK * side + t : PACK * side + t + 1],
                        scale=1.0,
                    )

        def affinity(r):
            grouped = []
            for i in range(ROUND_B):
                rows = planes[r][:, :, :, i, :].rearrange("p t s n -> p s t n")
                grouped.append(regroup(nc, work, rows, "grouped_batch%d" % i))
            for i in range(ROUND_B):
                codes, scales = quantise(nc, work, grouped[i], "batch%d" % i)
                prod = out_psum.tile([P, ROW_TILES, POINTS], F32, name="prod")
                for c in range(ROW_TILES):
                    rows_c = slice(P * c, P * (c + 1))
                    nc.tensor.matmul_mx(
                        out=prod[:, c, :],
                        lhsT=codes[:, 0, rows_c].bitcast(FP8X4),
                        lhsT_scale=scales[:, 0, rows_c],
                        rhs=codes[:, 1, :].bitcast(FP8X4),
                        rhs_scale=scales[:, 1, :],
                        start=True,
                        stop=True,
                    )
                result = result_pool.tile([P, ROW_TILES, POINTS], F32, name="result")
                nc.scalar.activation(out=result[:], in_=prod[:], func=ACT.Copy, scale=1.0 / POINTS)
                nc.sync.dma_start(out=out[ROUND_B * r + i].rearrange("(c p) m -> p c m", p=P), in_=result[:])

        with tc.manual_schedule():
            scalar_regroups(0)
            for r in range(LEAD):
                quantise_inputs(r)
                project(r)
                scalar_regroups(r + 1)
            for r in range(LEAD + 1, SCALAR_LEAD):
                scalar_regroups(r)
            for r in range(ROUNDS):
                load_round(r + LOADS_AHEAD)
                if r + LEAD < ROUNDS:
                    quantise_inputs(r + LEAD)
                    project(r + LEAD)
                affinity(r)
                scalar_regroups(r + SCALAR_LEAD)
